import numpy as np
import ml_dtypes


def mxq(x, axis, fmt="e4m3"):
    dtype, down = {"e4m3": (ml_dtypes.float8_e4m3fn, 7), "e5m2": (ml_dtypes.float8_e5m2, 14)}[fmt]
    v = np.moveaxis(np.asarray(x, np.float32).astype(ml_dtypes.bfloat16).astype(np.float64), axis, -1)
    blocks = v.reshape(v.shape[:-1] + (-1, 32))
    amax = np.abs(blocks).max(-1, keepdims=True)
    byte = np.maximum(np.where(amax > 0, np.frexp(amax)[1] - 1 + 127, 0) - down, 1)
    scale = np.exp2(byte - 127.0)
    codes = (blocks / scale).astype(np.float32).astype(dtype).astype(np.float64)
    return np.moveaxis((codes * scale).reshape(v.shape), -1, axis)


WIDE = False


def mx_kscale(k):
    if not WIDE:
        return np.ones(k)
    levels = np.array([10, -10, 5, -5, 0])
    a = np.random.permutation(np.resize(levels, k // 512 * 4)).reshape(k // 512, 4)
    idx = np.arange(k)
    return np.exp2(a[idx // 512, idx % 128 // 32])


BF16 = ml_dtypes.bfloat16


def bf(x):
    return np.asarray(x, np.float32).astype(BF16)


def f64(x):
    return np.asarray(x).astype(np.float64)


E2M1 = np.array([0.0, 0.5, 1.0, 1.5, 2.0, 3.0, 4.0, 6.0, -0.0, -0.5, -1.0, -1.5, -2.0, -3.0, -4.0, -6.0])


def pack_weight(w, fmt):
    k, n = w.shape
    w = f64(bf(w)).reshape(k // 32, 32, n)
    amax = np.abs(w).max(1)
    if fmt == "e4m3":
        byte = np.frexp(amax)[1] - 1 + 127 - 7
    else:
        mant, ex = np.frexp(amax / 6.0)
        byte = np.where(mant > 0.5, ex, ex - 1) + 127
    byte = np.clip(np.where(amax > 0, byte, 1), 1, 254)
    scaled = (w * np.exp2(127.0 - byte)[:, None, :]).reshape(k, n).astype(np.float32)
    by_word = np.ascontiguousarray(scaled.reshape(k // 512, 128, 4, n).transpose(0, 1, 3, 2))
    if fmt == "e4m3":
        words = by_word.astype(ml_dtypes.float8_e4m3fn).view(np.uint8)
    else:
        c = by_word.astype(ml_dtypes.float4_e2m1fn).view(np.uint8) & 0xF
        words = c[..., 0::2] | (c[..., 1::2] << 4)
    return np.ascontiguousarray(words), np.ascontiguousarray(byte.astype(np.uint8).reshape(k // 512, 16, n))


def unpack_weight(words, scales, fmt):
    g, p, n, _ = words.shape
    if fmt == "e4m3":
        vals = np.ascontiguousarray(words).view(ml_dtypes.float8_e4m3fn).astype(np.float64)
    else:
        nib = np.empty((g, p, n, 4), np.uint8)
        nib[..., 0::2] = words & 0xF
        nib[..., 1::2] = words >> 4
        vals = E2M1[nib]
    vals = vals * np.repeat(np.exp2(scales.astype(np.float64) - 127.0), 8, axis=1)[..., None]
    return vals.transpose(0, 1, 3, 2).reshape(g * 512, n)

def pack4(w):
    words, scales = pack_weight(w, "e2m1")
    return words.reshape(words.shape[0], 128, -1), scales


def unpack4(words, scales):
    return unpack_weight(words.reshape(words.shape[0], 128, -1, 2), scales, "e2m1")


B, D, H = 128, 1024, 2048
G = 4
QH = H % 512 == 0


def sigmoid(v):
    return 1.0 / (1.0 + np.exp(-v))


def setup_inputs():
    s = mx_kscale(D)
    t = mx_kscale(H) if QH else np.ones(H)
    x_t = bf(np.random.standard_normal((B, D)) * s)
    h_pre = bf(np.random.standard_normal((B, H)) * t)
    c_pre = bf(np.random.standard_normal((B, H)))
    Wx = np.random.standard_normal((G, H, D)) * 0.64 / np.sqrt(D) / s
    Wx_cat = np.ascontiguousarray(Wx.swapaxes(1, 2)).reshape(-1, H)
    Wx_words, Wx_scales = pack4(Wx_cat)
    bW = bf(np.random.standard_normal((4, H)) * 0.3)
    Uh = bf(np.random.standard_normal((4, H, H)) * 0.64 / np.sqrt(H) / t)
    bU = bf(np.random.standard_normal((4, H)) * 0.3)
    return {
        "x_t": x_t,
        "h_pre": h_pre,
        "c_pre": c_pre,
        "Wx_words": Wx_words,
        "Wx_scales": Wx_scales,
        "bW": bW,
        "Uh": Uh,
        "bU": bU,
    }


def reference(x_t, h_pre, c_pre, Wx_words, Wx_scales, bW, Uh, bU):
    zx = mxq(f64(x_t), 1, "e4m3") @ unpack4(Wx_words, Wx_scales).reshape(G, D, H)
    if QH:
        zh = mxq(f64(h_pre), 1, "e4m3") @ mxq(f64(Uh), 2, "e4m3").transpose(0, 2, 1)
    else:
        zh = f64(h_pre) @ f64(Uh).transpose(0, 2, 1)
    z = zx + zh + (f64(bW) + f64(bU))[:, None, :]
    f_t = sigmoid(z[0])
    i_t = sigmoid(z[1])
    o_t = sigmoid(z[2])
    g_t = np.tanh(z[3])
    c_t = f_t * f64(c_pre) + i_t * g_t
    h_t = o_t * np.tanh(c_t)
    return (h_t, c_t)

@@ -1,0 +1,327 @@
+from contextlib import ExitStack
+
+import concourse.mybir as mybir
+from concourse.masks import make_identity
+
+F32 = mybir.dt.float32
+BF16 = mybir.dt.bfloat16
+I32 = mybir.dt.int32
+U32 = mybir.dt.uint32
+U8 = mybir.dt.uint8
+FP8X4 = mybir.dt.float8_e4m3fn_x4
+FP4X4 = mybir.dt.float4_e2m1fn_x4
+ACT = mybir.ActivationFunctionType
+ALU = mybir.AluOpType
+
+P = 128
+D = 1024
+H = 2048
+GATES = 4
+K_PASS = 512
+X_PASSES = D // K_PASS
+H_PASSES = H // K_PASS
+WORDS_PER_PASS = K_PASS // 2
+
+N_TILE = 512
+CHUNKS = H // N_TILE
+UNITS = GATES * CHUNKS
+ROWS_PER_PARTITION = 2
+PIECE_ROWS = P * ROWS_PER_PARTITION
+PIECES_PER_UNIT = N_TILE // PIECE_ROWS
+PIECES = UNITS * PIECES_PER_UNIT
+PIECES_PER_GATE = PIECES // GATES
+
+GATE_ORDER = (3, 1, 0, 2)
+STEP_G, STEP_I, STEP_F, STEP_O = 0, 1, 2, 3
+
+RAW_BUFS = 8
+TRANSPOSE_BANKS = 7
+SCALAR_BANKS = 3
+
+FLOPS = 2 * P * (D + H) * GATES * H
+
+
+def tile_lstmcell_w_e_kernel(
+    tc, x_t, h_pre, c_pre, Wx_words, Wx_scales, bW, Uh, bU, out_0, out_1
+):
+    nc = tc.nc
+    with ExitStack() as ctx:
+        ctx.enter_context(tc.manual_schedule())
+        const = ctx.enter_context(tc.tile_pool(name="const", bufs=1))
+        raw_pool = ctx.enter_context(tc.tile_pool(name="raw", bufs=RAW_BUFS))
+        grouped_pool = ctx.enter_context(tc.tile_pool(name="grouped", bufs=2 * H_PASSES))
+        codes_pool = ctx.enter_context(tc.tile_pool(name="codes", bufs=2))
+        wx_pool = ctx.enter_context(tc.tile_pool(name="wx", bufs=2))
+        work = ctx.enter_context(tc.tile_pool(name="work", bufs=2))
+        banks = ctx.enter_context(tc.psum_pool(name="banks", bufs=TRANSPOSE_BANKS))
+        z_pool = ctx.enter_context(tc.psum_pool(name="z", bufs=1))
+
+        ident = const.tile([P, P], F32)
+        make_identity(nc, ident[:])
+
+        bias_rows = const.tile([P, N_TILE], BF16)
+        nc.vector.memset(bias_rows[:], 0.0)
+        wx_planes = const.tile([P, GATES * X_PASSES, H], U8, align_bytes=64)
+        nc.vector.memset(wx_planes[:].bitcast(I32), 0)
+        pick = const.tile([P, UNITS], BF16)
+        nc.vector.tensor_tensor(
+            out=pick[:], in0=ident[:, 0:UNITS], in1=ident[:, UNITS : 2 * UNITS], op=ALU.add
+        )
+
+        nc.sync.dma_start(
+            out=bias_rows[0:UNITS, :], in_=bW.rearrange("e (c n) -> (e c) n", n=N_TILE)
+        )
+        nc.sync.dma_start(
+            out=bias_rows[UNITS : 2 * UNITS, :], in_=bU.rearrange("e (c n) -> (e c) n", n=N_TILE)
+        )
+        h_raw = const.tile([P, H], BF16)
+        nc.sync.dma_start(out=h_raw[:], in_=h_pre[:, :])
+        x_raw = const.tile([P, D], BF16)
+        nc.sync.dma_start(out=x_raw[:], in_=x_t[:, :])
+        c_old = const.tile([P, H], BF16)
+
+        warm = const.tile([P, 1], F32)
+        nc.scalar.activation(out=warm[:], in_=ident[:, 0:1], func=ACT.Sigmoid)
+
+        cell = const.tile([P, H], F32)
+        tanh_cell = const.tile([P, H], F32)
+
+        raw_of = {}
+        grouped_of = {}
+        codes_of = {}
+        scales_of = {}
+        wx_words_of = {}
+        bias_bank_of = {}
+        bias_of = {}
+        z_of = {}
+        z_biased_of = {}
+        gate_of = {}
+
+        def unit_place(unit):
+            step, chunk = divmod(unit, CHUNKS)
+            return step, GATE_ORDER[step], chunk * N_TILE
+
+        def load_piece(piece):
+            step, rest = divmod(piece, PIECES_PER_GATE)
+            rows = slice(rest * PIECE_ROWS, (rest + 1) * PIECE_ROWS)
+            raw = raw_pool.tile([P, ROWS_PER_PARTITION, H], BF16)
+            nc.sync.dma_start(
+                out=raw[:],
+                in_=Uh[GATE_ORDER[step], rows, :].rearrange(
+                    "(p t) k -> p t k", t=ROWS_PER_PARTITION
+                ),
+            )
+            raw_of[piece] = raw
+
+        def load_gate_weights(step):
+            first = GATE_ORDER[step] * X_PASSES
+            groups = slice(first, first + X_PASSES)
+            for quadrant in range(4):
+                nc.sync.dma_start(
+                    out=wx_planes[32 * quadrant : 32 * quadrant + 4, groups, :].bitcast(I32),
+                    in_=Wx_scales[groups, 4 * quadrant : 4 * quadrant + 4, :]
+                    .bitcast(I32)
+                    .rearrange("g r w -> r g w"),
+                )
+            wx_words = wx_pool.tile([P, X_PASSES, 2 * H], U8, align_bytes=64)
+            nc.sync.dma_start(
+                out=wx_words[:].bitcast(I32),
+                in_=Wx_words[groups, :, :].bitcast(I32).rearrange("g p w -> p g w"),
+            )
+            wx_words_of[step] = wx_words
+
+        def quantise_activations(raw, passes, word_columns, codes, scales, grouped):
+            raw_words = raw[:].bitcast(F32)
+            grouped_words = grouped[:].bitcast(F32).rearrange(
+                "q (g b u) -> q g b u", g=passes, u=2
+            )
+            for pair in range(passes // 2):
+                bank = banks.tile([P, 4, P], F32)
+                for g in range(2):
+                    for u in range(2):
+                        nc.tensor.transpose(
+                            out=bank[:, 2 * g + u, :],
+                            in_=raw_words[:, word_columns(2 * pair + g, u)],
+                            identity=ident[:],
+                        )
+                nc.scalar.copy(
+                    out=grouped_words[:, 2 * pair : 2 * pair + 2, :, :],
+                    in_=bank[:].rearrange("q (g u) b -> q g b u", u=2),
+                )
+            nc.vector.quantize_mx(
+                out=codes[:].rearrange("q g b -> q (g b)").bitcast(FP8X4),
+                scales=scales[:].rearrange("q g b -> q (g b)"),
+                in_=grouped[:],
+            )
+
+        h_codes = const.tile([P, H_PASSES, P], U32, align_bytes=64)
+        h_scales = const.tile([P, H_PASSES, P], U8, align_bytes=64)
+        h_grouped = const.tile([P, H_PASSES * P * 4], BF16, align_bytes=64)
+        x_codes = const.tile([P, X_PASSES, P], U32, align_bytes=64)
+        x_scales = const.tile([P, X_PASSES, P], U8, align_bytes=64)
+        x_grouped = const.tile([P, X_PASSES * P * 4], BF16, align_bytes=64)
+
+        def h_word_columns(g, u):
+            first = WORDS_PER_PASS * g + P * u
+            return slice(first, first + P)
+
+        def x_word_columns(g, u):
+            return slice(WORDS_PER_PASS * g + u, WORDS_PER_PASS * (g + 1), 2)
+
+        def transpose_piece(piece):
+            raw_words = raw_of[piece][:].bitcast(F32)
+            for g in range(H_PASSES):
+                bank = banks.tile([P, 4, P], F32)
+                for t in range(ROWS_PER_PARTITION):
+                    for u in range(2):
+                        nc.tensor.transpose(
+                            out=bank[:, 2 * t + u, :],
+                            in_=raw_words[:, t, h_word_columns(g, u)],
+                            identity=ident[:],
+                        )
+                grouped = grouped_pool.tile([P, PIECE_ROWS * 4], BF16, align_bytes=64)
+                copy = nc.scalar.copy if g < SCALAR_BANKS else nc.vector.tensor_copy
+                copy(
+                    out=grouped[:].bitcast(F32).rearrange("q (p c) -> q p c", c=4),
+                    in_=bank[:].rearrange("q c p -> q p c"),
+                )
+                grouped_of[(piece, g)] = grouped
+
+        def quantise_piece(piece):
+            unit, half = divmod(piece, PIECES_PER_UNIT)
+            if half == 0:
+                codes = codes_pool.tile([P, H_PASSES, N_TILE], U32, align_bytes=64)
+                scales = codes_pool.tile([P, H_PASSES, N_TILE], U8, align_bytes=64)
+                codes_of[unit] = codes
+                scales_of[unit] = scales
+            columns = slice(half * PIECE_ROWS, (half + 1) * PIECE_ROWS)
+            for g in range(H_PASSES):
+                nc.vector.quantize_mx(
+                    out=codes_of[unit][:, g, columns].bitcast(FP8X4),
+                    scales=scales_of[unit][:, g, columns],
+                    in_=grouped_of[(piece, g)][:],
+                )
+
+        def spread_bias(unit):
+            step, gate, first = unit_place(unit)
+            row = gate * CHUNKS + first // N_TILE
+            bank = banks.tile([P, 4, P], F32)
+            nc.tensor.matmul(
+                out=bank[:].rearrange("q c p -> q (c p)"),
+                lhsT=pick[:, row : row + 1].to_broadcast([P, P]),
+                rhs=bias_rows[:],
+                start=True,
+                stop=True,
+            )
+            bias_bank_of[unit] = bank
+
+        def fetch_bias(unit):
+            bias = work.tile([P, N_TILE], F32)
+            nc.scalar.copy(out=bias[:], in_=bias_bank_of[unit][:].rearrange("q c p -> q (c p)"))
+            bias_of[unit] = bias
+
+        def multiply(unit):
+            step, gate, first = unit_place(unit)
+            z = z_pool.tile([P, N_TILE], F32)
+            for g in range(X_PASSES):
+                nc.tensor.matmul_mx(
+                    out=z[:],
+                    lhsT=x_codes[:, g, :].bitcast(FP8X4),
+                    lhsT_scale=x_scales[:, g, :],
+                    rhs=wx_words_of[step][:, g, 2 * first : 2 * (first + N_TILE)].bitcast(FP4X4),
+                    rhs_scale=wx_planes[:, gate * X_PASSES + g, first : first + N_TILE],
+                    start=(g == 0),
+                    stop=False,
+                )
+            for g in range(H_PASSES):
+                nc.tensor.matmul_mx(
+                    out=z[:],
+                    lhsT=h_codes[:, g, :].bitcast(FP8X4),
+                    lhsT_scale=h_scales[:, g, :],
+                    rhs=codes_of[unit][:, g, :].bitcast(FP8X4),
+                    rhs_scale=scales_of[unit][:, g, :],
+                    start=False,
+                    stop=(g == H_PASSES - 1),
+                )
+            z_of[unit] = z
+
+        def add_bias(unit):
+            z_biased = work.tile([P, N_TILE], F32)
+            nc.vector.tensor_tensor(
+                out=z_biased[:], in0=z_of[unit][:], in1=bias_of[unit][:], op=ALU.add
+            )
+            z_biased_of[unit] = z_biased
+
+        def activate(unit):
+            step, gate, first = unit_place(unit)
+            columns = slice(first, first + N_TILE)
+            if step == STEP_G:
+                nc.scalar.activation(out=cell[:, columns], in_=z_biased_of[unit][:], func=ACT.Tanh)
+            else:
+                gate_value = work.tile([P, N_TILE], F32)
+                nc.scalar.activation(out=gate_value[:], in_=z_biased_of[unit][:], func=ACT.Sigmoid)
+                gate_of[unit] = gate_value
+
+        def update_cell(unit):
+            step, gate, first = unit_place(unit)
+            columns = slice(first, first + N_TILE)
+            if step == STEP_I:
+                nc.vector.tensor_tensor(
+                    out=cell[:, columns], in0=gate_of[unit][:], in1=cell[:, columns], op=ALU.mult
+                )
+            if step == STEP_F:
+                kept = work.tile([P, N_TILE], F32)
+                nc.vector.tensor_tensor(
+                    out=kept[:], in0=gate_of[unit][:], in1=c_old[:, columns], op=ALU.mult
+                )
+                nc.vector.tensor_tensor(
+                    out=cell[:, columns], in0=kept[:], in1=cell[:, columns], op=ALU.add
+                )
+                nc.sync.dma_start(out=out_1[:, columns], in_=cell[:, columns])
+            if step == STEP_O:
+                h_new = work.tile([P, N_TILE], F32)
+                nc.vector.tensor_tensor(
+                    out=h_new[:], in0=gate_of[unit][:], in1=tanh_cell[:, columns], op=ALU.mult
+                )
+                nc.sync.dma_start(out=out_0[:, columns], in_=h_new[:])
+
+        def squash_cell(unit):
+            step, gate, first = unit_place(unit)
+            columns = slice(first, first + N_TILE)
+            if step == STEP_F:
+                nc.scalar.activation(out=tanh_cell[:, columns], in_=cell[:, columns], func=ACT.Tanh)
+
+        for piece in range(RAW_BUFS):
+            if piece == PIECES_PER_UNIT:
+                load_gate_weights(0)
+            load_piece(piece)
+        nc.sync.dma_start(out=c_old[:], in_=c_pre[:, :])
+
+        quantise_activations(h_raw, H_PASSES, h_word_columns, h_codes, h_scales, h_grouped)
+        quantise_activations(x_raw, X_PASSES, x_word_columns, x_codes, x_scales, x_grouped)
+        spread_bias(0)
+
+        for r in range(PIECES + 4):
+            even = r % 2 == 0
+            if even and 0 <= (r - 4) // 2 < UNITS:
+                activate((r - 4) // 2)
+            if not even and (r - 1) // 2 < UNITS:
+                fetch_bias((r - 1) // 2)
+            if not even and 0 <= (r - 5) // 2 < UNITS:
+                squash_cell((r - 5) // 2)
+            if 1 <= r <= PIECES:
+                quantise_piece(r - 1)
+            if r < PIECES:
+                transpose_piece(r)
+            if even and 0 <= r // 2 - 1 < UNITS:
+                multiply(r // 2 - 1)
+                if r // 2 < UNITS:
+                    spread_bias(r // 2)
+            if not even and 0 <= (r - 3) // 2 < UNITS:
+                add_bias((r - 3) // 2)
+            if even and 0 <= (r - 4) // 2 < UNITS:
+                update_cell((r - 4) // 2)
+            if r + RAW_BUFS < PIECES:
+                if (r + RAW_BUFS) % PIECES_PER_GATE == 0:
+                    load_gate_weights((r + RAW_BUFS) // PIECES_PER_GATE)
+                load_piece(r + RAW_BUFS)

@@ -53,6 +53,7 @@ def tile_lstmcell_w_e_kernel(
         codes_pool = ctx.enter_context(tc.tile_pool(name="codes", bufs=2))
         wx_pool = ctx.enter_context(tc.tile_pool(name="wx", bufs=2))
         work = ctx.enter_context(tc.tile_pool(name="work", bufs=2))
+        bias_pool = ctx.enter_context(tc.tile_pool(name="bias", bufs=2 * CHUNKS))
         banks = ctx.enter_context(tc.psum_pool(name="banks", bufs=TRANSPOSE_BANKS))
         z_pool = ctx.enter_context(tc.psum_pool(name="z", bufs=1))
 
@@ -68,16 +69,16 @@ def tile_lstmcell_w_e_kernel(
             out=pick[:], in0=ident[:, 0:UNITS], in1=ident[:, UNITS : 2 * UNITS], op=ALU.add
         )
 
+        h_raw = const.tile([P, H], BF16)
+        nc.sync.dma_start(out=h_raw[:], in_=h_pre[:, :])
+        x_raw = const.tile([P, D], BF16)
+        nc.sync.dma_start(out=x_raw[:], in_=x_t[:, :])
         nc.sync.dma_start(
             out=bias_rows[0:UNITS, :], in_=bW.rearrange("e (c n) -> (e c) n", n=N_TILE)
         )
         nc.sync.dma_start(
             out=bias_rows[UNITS : 2 * UNITS, :], in_=bU.rearrange("e (c n) -> (e c) n", n=N_TILE)
         )
-        h_raw = const.tile([P, H], BF16)
-        nc.sync.dma_start(out=h_raw[:], in_=h_pre[:, :])
-        x_raw = const.tile([P, D], BF16)
-        nc.sync.dma_start(out=x_raw[:], in_=x_t[:, :])
         c_old = const.tile([P, H], BF16)
 
         warm = const.tile([P, 1], F32)
@@ -216,7 +217,7 @@ def tile_lstmcell_w_e_kernel(
             bias_bank_of[unit] = bank
 
         def fetch_bias(unit):
-            bias = work.tile([P, N_TILE], F32)
+            bias = bias_pool.tile([P, N_TILE], F32)
             nc.scalar.copy(out=bias[:], in_=bias_bank_of[unit][:].rearrange("q c p -> q (c p)"))
             bias_of[unit] = bias
 
@@ -299,28 +300,41 @@ def tile_lstmcell_w_e_kernel(
 
         quantise_activations(h_raw, H_PASSES, h_word_columns, h_codes, h_scales, h_grouped)
         quantise_activations(x_raw, X_PASSES, x_word_columns, x_codes, x_scales, x_grouped)
-        spread_bias(0)
+
+        def prepare_gate_bias(step):
+            for unit in range(step * CHUNKS, (step + 1) * CHUNKS):
+                spread_bias(unit)
+            for unit in range(step * CHUNKS, (step + 1) * CHUNKS):
+                fetch_bias(unit)
+
+        def unit_due(r, lag):
+            unit, rest = divmod(r - lag, PIECES_PER_UNIT)
+            return unit if rest == 0 and 0 <= unit < UNITS else None
+
+        prepare_gate_bias(0)
 
         for r in range(PIECES + 4):
-            even = r % 2 == 0
-            if even and 0 <= (r - 4) // 2 < UNITS:
-                activate((r - 4) // 2)
-            if not even and (r - 1) // 2 < UNITS:
-                fetch_bias((r - 1) // 2)
-            if not even and 0 <= (r - 5) // 2 < UNITS:
-                squash_cell((r - 5) // 2)
+            unit = unit_due(r, 4)
+            if unit is not None:
+                activate(unit)
+            unit = unit_due(r, 5)
+            if unit is not None:
+                squash_cell(unit)
             if 1 <= r <= PIECES:
                 quantise_piece(r - 1)
+            unit = unit_due(r, 3)
+            if unit is not None:
+                add_bias(unit)
+            unit = unit_due(r, 4)
+            if unit is not None:
+                update_cell(unit)
             if r < PIECES:
                 transpose_piece(r)
-            if even and 0 <= r // 2 - 1 < UNITS:
-                multiply(r // 2 - 1)
-                if r // 2 < UNITS:
-                    spread_bias(r // 2)
-            if not even and 0 <= (r - 3) // 2 < UNITS:
-                add_bias((r - 3) // 2)
-            if even and 0 <= (r - 4) // 2 < UNITS:
-                update_cell((r - 4) // 2)
+            unit = unit_due(r, 2)
+            if unit is not None:
+                multiply(unit)
+            if (r + 1) % PIECES_PER_GATE == 0 and r + 1 < PIECES:
+                prepare_gate_bias((r + 1) // PIECES_PER_GATE)
             if r + RAW_BUFS < PIECES:
                 if (r + RAW_BUFS) % PIECES_PER_GATE == 0:
                     load_gate_weights((r + RAW_BUFS) // PIECES_PER_GATE)

@@ -109,7 +109,7 @@ def tile_lstmcell_w_e_kernel(
             nc.sync.dma_start(
                 out=raw[:],
                 in_=Uh[GATE_ORDER[step], rows, :].rearrange(
-                    "(p t) k -> p t k", t=ROWS_PER_PARTITION
+                    "(t p) k -> p t k", t=ROWS_PER_PARTITION
                 ),
             )
             raw_of[piece] = raw
@@ -183,8 +183,10 @@ def tile_lstmcell_w_e_kernel(
                 grouped = grouped_pool.tile([P, PIECE_ROWS * 4], BF16, align_bytes=64)
                 copy = nc.scalar.copy if g < SCALAR_BANKS else nc.vector.tensor_copy
                 copy(
-                    out=grouped[:].bitcast(F32).rearrange("q (p c) -> q p c", c=4),
-                    in_=bank[:].rearrange("q c p -> q p c"),
+                    out=grouped[:].bitcast(F32).rearrange(
+                        "q (t p u) -> q t p u", t=ROWS_PER_PARTITION, u=2
+                    ),
+                    in_=bank[:].rearrange("q (t u) p -> q t p u", u=2),
                 )
                 grouped_of[(piece, g)] = grouped
 

from contextlib import ExitStack

import concourse.mybir as mybir
from concourse.masks import make_identity

F32 = mybir.dt.float32
BF16 = mybir.dt.bfloat16
I32 = mybir.dt.int32
U32 = mybir.dt.uint32
U8 = mybir.dt.uint8
FP8X4 = mybir.dt.float8_e4m3fn_x4
FP4X4 = mybir.dt.float4_e2m1fn_x4
ACT = mybir.ActivationFunctionType
ALU = mybir.AluOpType

P = 128
D = 1024
H = 2048
GATES = 4
K_PASS = 512
X_PASSES = D // K_PASS
H_PASSES = H // K_PASS
WORDS_PER_PASS = K_PASS // 2

N_TILE = 512
CHUNKS = H // N_TILE
UNITS = GATES * CHUNKS
ROWS_PER_PARTITION = 2
PIECE_ROWS = P * ROWS_PER_PARTITION
PIECES_PER_UNIT = N_TILE // PIECE_ROWS
PIECES = UNITS * PIECES_PER_UNIT
PIECES_PER_GATE = PIECES // GATES

GATE_ORDER = (3, 1, 0, 2)
STEP_G, STEP_I, STEP_F, STEP_O = 0, 1, 2, 3

RAW_BUFS = 8
TRANSPOSE_BANKS = 7
SCALAR_BANKS = 3

FLOPS = 2 * P * (D + H) * GATES * H


def tile_lstmcell_w_e_kernel(
    tc, x_t, h_pre, c_pre, Wx_words, Wx_scales, bW, Uh, bU, out_0, out_1
):
    nc = tc.nc
    with ExitStack() as ctx:
        ctx.enter_context(tc.manual_schedule())
        const = ctx.enter_context(tc.tile_pool(name="const", bufs=1))
        raw_pool = ctx.enter_context(tc.tile_pool(name="raw", bufs=RAW_BUFS))
        grouped_pool = ctx.enter_context(tc.tile_pool(name="grouped", bufs=2 * H_PASSES))
        codes_pool = ctx.enter_context(tc.tile_pool(name="codes", bufs=2))
        wx_pool = ctx.enter_context(tc.tile_pool(name="wx", bufs=2))
        work = ctx.enter_context(tc.tile_pool(name="work", bufs=2))
        bias_pool = ctx.enter_context(tc.tile_pool(name="bias", bufs=2 * CHUNKS))
        banks = ctx.enter_context(tc.psum_pool(name="banks", bufs=TRANSPOSE_BANKS))
        z_pool = ctx.enter_context(tc.psum_pool(name="z", bufs=1))

        ident = const.tile([P, P], F32)
        make_identity(nc, ident[:])

        bias_rows = const.tile([P, N_TILE], BF16)
        nc.vector.memset(bias_rows[:], 0.0)
        wx_planes = const.tile([P, GATES * X_PASSES, H], U8, align_bytes=64)
        nc.vector.memset(wx_planes[:].bitcast(I32), 0)
        pick = const.tile([P, UNITS], BF16)
        nc.vector.tensor_tensor(
            out=pick[:], in0=ident[:, 0:UNITS], in1=ident[:, UNITS : 2 * UNITS], op=ALU.add
        )

        h_raw = const.tile([P, H], BF16)
        nc.sync.dma_start(out=h_raw[:], in_=h_pre[:, :])
        x_raw = const.tile([P, D], BF16)
        nc.sync.dma_start(out=x_raw[:], in_=x_t[:, :])
        nc.sync.dma_start(
            out=bias_rows[0:UNITS, :], in_=bW.rearrange("e (c n) -> (e c) n", n=N_TILE)
        )
        nc.sync.dma_start(
            out=bias_rows[UNITS : 2 * UNITS, :], in_=bU.rearrange("e (c n) -> (e c) n", n=N_TILE)
        )
        c_old = const.tile([P, H], BF16)

        warm = const.tile([P, 1], F32)
        nc.scalar.activation(out=warm[:], in_=ident[:, 0:1], func=ACT.Sigmoid)

        cell = const.tile([P, H], F32)
        tanh_cell = const.tile([P, H], F32)

        raw_of = {}
        grouped_of = {}
        codes_of = {}
        scales_of = {}
        wx_words_of = {}
        bias_bank_of = {}
        bias_of = {}
        z_of = {}
        z_biased_of = {}
        gate_of = {}

        def unit_place(unit):
            step, chunk = divmod(unit, CHUNKS)
            return step, GATE_ORDER[step], chunk * N_TILE

        def load_piece(piece):
            step, rest = divmod(piece, PIECES_PER_GATE)
            rows = slice(rest * PIECE_ROWS, (rest + 1) * PIECE_ROWS)
            raw = raw_pool.tile([P, ROWS_PER_PARTITION, H], BF16)
            nc.sync.dma_start(
                out=raw[:],
                in_=Uh[GATE_ORDER[step], rows, :].rearrange(
                    "(t p) k -> p t k", t=ROWS_PER_PARTITION
                ),
            )
            raw_of[piece] = raw

        def load_gate_weights(step):
            first = GATE_ORDER[step] * X_PASSES
            groups = slice(first, first + X_PASSES)
            for quadrant in range(4):
                nc.sync.dma_start(
                    out=wx_planes[32 * quadrant : 32 * quadrant + 4, groups, :].bitcast(I32),
                    in_=Wx_scales[groups, 4 * quadrant : 4 * quadrant + 4, :]
                    .bitcast(I32)
                    .rearrange("g r w -> r g w"),
                )
            wx_words = wx_pool.tile([P, X_PASSES, 2 * H], U8, align_bytes=64)
            nc.sync.dma_start(
                out=wx_words[:].bitcast(I32),
                in_=Wx_words[groups, :, :].bitcast(I32).rearrange("g p w -> p g w"),
            )
            wx_words_of[step] = wx_words

        def quantise_activations(raw, passes, word_columns, codes, scales, grouped):
            raw_words = raw[:].bitcast(F32)
            grouped_words = grouped[:].bitcast(F32).rearrange(
                "q (g b u) -> q g b u", g=passes, u=2
            )
            for pair in range(passes // 2):
                bank = banks.tile([P, 4, P], F32)
                for g in range(2):
                    for u in range(2):
                        nc.tensor.transpose(
                            out=bank[:, 2 * g + u, :],
                            in_=raw_words[:, word_columns(2 * pair + g, u)],
                            identity=ident[:],
                        )
                nc.scalar.copy(
                    out=grouped_words[:, 2 * pair : 2 * pair + 2, :, :],
                    in_=bank[:].rearrange("q (g u) b -> q g b u", u=2),
                )
            nc.vector.quantize_mx(
                out=codes[:].rearrange("q g b -> q (g b)").bitcast(FP8X4),
                scales=scales[:].rearrange("q g b -> q (g b)"),
                in_=grouped[:],
            )

        h_codes = const.tile([P, H_PASSES, P], U32, align_bytes=64)
        h_scales = const.tile([P, H_PASSES, P], U8, align_bytes=64)
        h_grouped = const.tile([P, H_PASSES * P * 4], BF16, align_bytes=64)
        x_codes = const.tile([P, X_PASSES, P], U32, align_bytes=64)
        x_scales = const.tile([P, X_PASSES, P], U8, align_bytes=64)
        x_grouped = const.tile([P, X_PASSES * P * 4], BF16, align_bytes=64)

        def h_word_columns(g, u):
            first = WORDS_PER_PASS * g + P * u
            return slice(first, first + P)

        def x_word_columns(g, u):
            return slice(WORDS_PER_PASS * g + u, WORDS_PER_PASS * (g + 1), 2)

        def transpose_piece(piece):
            raw_words = raw_of[piece][:].bitcast(F32)
            for g in range(H_PASSES):
                bank = banks.tile([P, 4, P], F32)
                for t in range(ROWS_PER_PARTITION):
                    for u in range(2):
                        nc.tensor.transpose(
                            out=bank[:, 2 * t + u, :],
                            in_=raw_words[:, t, h_word_columns(g, u)],
                            identity=ident[:],
                        )
                grouped = grouped_pool.tile([P, PIECE_ROWS * 4], BF16, align_bytes=64)
                copy = nc.scalar.copy if g < SCALAR_BANKS else nc.vector.tensor_copy
                copy(
                    out=grouped[:].bitcast(F32).rearrange(
                        "q (t p u) -> q t p u", t=ROWS_PER_PARTITION, u=2
                    ),
                    in_=bank[:].rearrange("q (t u) p -> q t p u", u=2),
                )
                grouped_of[(piece, g)] = grouped

        def quantise_piece(piece):
            unit, half = divmod(piece, PIECES_PER_UNIT)
            if half == 0:
                codes = codes_pool.tile([P, H_PASSES, N_TILE], U32, align_bytes=64)
                scales = codes_pool.tile([P, H_PASSES, N_TILE], U8, align_bytes=64)
                codes_of[unit] = codes
                scales_of[unit] = scales
            columns = slice(half * PIECE_ROWS, (half + 1) * PIECE_ROWS)
            for g in range(H_PASSES):
                nc.vector.quantize_mx(
                    out=codes_of[unit][:, g, columns].bitcast(FP8X4),
                    scales=scales_of[unit][:, g, columns],
                    in_=grouped_of[(piece, g)][:],
                )

        def spread_bias(unit):
            step, gate, first = unit_place(unit)
            row = gate * CHUNKS + first // N_TILE
            bank = banks.tile([P, 4, P], F32)
            nc.tensor.matmul(
                out=bank[:].rearrange("q c p -> q (c p)"),
                lhsT=pick[:, row : row + 1].to_broadcast([P, P]),
                rhs=bias_rows[:],
                start=True,
                stop=True,
            )
            bias_bank_of[unit] = bank

        def fetch_bias(unit):
            bias = bias_pool.tile([P, N_TILE], F32)
            nc.scalar.copy(out=bias[:], in_=bias_bank_of[unit][:].rearrange("q c p -> q (c p)"))
            bias_of[unit] = bias

        def multiply(unit):
            step, gate, first = unit_place(unit)
            z = z_pool.tile([P, N_TILE], F32)
            for g in range(X_PASSES):
                nc.tensor.matmul_mx(
                    out=z[:],
                    lhsT=x_codes[:, g, :].bitcast(FP8X4),
                    lhsT_scale=x_scales[:, g, :],
                    rhs=wx_words_of[step][:, g, 2 * first : 2 * (first + N_TILE)].bitcast(FP4X4),
                    rhs_scale=wx_planes[:, gate * X_PASSES + g, first : first + N_TILE],
                    start=(g == 0),
                    stop=False,
                )
            for g in range(H_PASSES):
                nc.tensor.matmul_mx(
                    out=z[:],
                    lhsT=h_codes[:, g, :].bitcast(FP8X4),
                    lhsT_scale=h_scales[:, g, :],
                    rhs=codes_of[unit][:, g, :].bitcast(FP8X4),
                    rhs_scale=scales_of[unit][:, g, :],
                    start=False,
                    stop=(g == H_PASSES - 1),
                )
            z_of[unit] = z

        def add_bias(unit):
            z_biased = work.tile([P, N_TILE], F32)
            nc.vector.tensor_tensor(
                out=z_biased[:], in0=z_of[unit][:], in1=bias_of[unit][:], op=ALU.add
            )
            z_biased_of[unit] = z_biased

        def activate(unit):
            step, gate, first = unit_place(unit)
            columns = slice(first, first + N_TILE)
            if step == STEP_G:
                nc.scalar.activation(out=cell[:, columns], in_=z_biased_of[unit][:], func=ACT.Tanh)
            else:
                gate_value = work.tile([P, N_TILE], F32)
                nc.scalar.activation(out=gate_value[:], in_=z_biased_of[unit][:], func=ACT.Sigmoid)
                gate_of[unit] = gate_value

        def update_cell(unit):
            step, gate, first = unit_place(unit)
            columns = slice(first, first + N_TILE)
            if step == STEP_I:
                nc.vector.tensor_tensor(
                    out=cell[:, columns], in0=gate_of[unit][:], in1=cell[:, columns], op=ALU.mult
                )
            if step == STEP_F:
                kept = work.tile([P, N_TILE], F32)
                nc.vector.tensor_tensor(
                    out=kept[:], in0=gate_of[unit][:], in1=c_old[:, columns], op=ALU.mult
                )
                nc.vector.tensor_tensor(
                    out=cell[:, columns], in0=kept[:], in1=cell[:, columns], op=ALU.add
                )
                nc.sync.dma_start(out=out_1[:, columns], in_=cell[:, columns])
            if step == STEP_O:
                h_new = work.tile([P, N_TILE], F32)
                nc.vector.tensor_tensor(
                    out=h_new[:], in0=gate_of[unit][:], in1=tanh_cell[:, columns], op=ALU.mult
                )
                nc.sync.dma_start(out=out_0[:, columns], in_=h_new[:])

        def squash_cell(unit):
            step, gate, first = unit_place(unit)
            columns = slice(first, first + N_TILE)
            if step == STEP_F:
                nc.scalar.activation(out=tanh_cell[:, columns], in_=cell[:, columns], func=ACT.Tanh)

        for piece in range(RAW_BUFS):
            if piece == PIECES_PER_UNIT:
                load_gate_weights(0)
            load_piece(piece)
        nc.sync.dma_start(out=c_old[:], in_=c_pre[:, :])

        quantise_activations(h_raw, H_PASSES, h_word_columns, h_codes, h_scales, h_grouped)
        quantise_activations(x_raw, X_PASSES, x_word_columns, x_codes, x_scales, x_grouped)

        def prepare_gate_bias(step):
            for unit in range(step * CHUNKS, (step + 1) * CHUNKS):
                spread_bias(unit)
            for unit in range(step * CHUNKS, (step + 1) * CHUNKS):
                fetch_bias(unit)

        def unit_due(r, lag):
            unit, rest = divmod(r - lag, PIECES_PER_UNIT)
            return unit if rest == 0 and 0 <= unit < UNITS else None

        prepare_gate_bias(0)

        for r in range(PIECES + 4):
            unit = unit_due(r, 4)
            if unit is not None:
                activate(unit)
            unit = unit_due(r, 5)
            if unit is not None:
                squash_cell(unit)
            if 1 <= r <= PIECES:
                quantise_piece(r - 1)
            unit = unit_due(r, 3)
            if unit is not None:
                add_bias(unit)
            unit = unit_due(r, 4)
            if unit is not None:
                update_cell(unit)
            if r < PIECES:
                transpose_piece(r)
            unit = unit_due(r, 2)
            if unit is not None:
                multiply(unit)
            if (r + 1) % PIECES_PER_GATE == 0 and r + 1 < PIECES:
                prepare_gate_bias((r + 1) // PIECES_PER_GATE)
            if r + RAW_BUFS < PIECES:
                if (r + RAW_BUFS) % PIECES_PER_GATE == 0:
                    load_gate_weights((r + RAW_BUFS) // PIECES_PER_GATE)
                load_piece(r + RAW_BUFS)
